import numpy as np
import ml_dtypes


def mxq(x, axis, fmt="e4m3"):
    dtype, down = {"e4m3": (ml_dtypes.float8_e4m3fn, 7), "e5m2": (ml_dtypes.float8_e5m2, 14)}[fmt]
    v = np.moveaxis(np.asarray(x, np.float32).astype(ml_dtypes.bfloat16).astype(np.float64), axis, -1)
    blocks = v.reshape(v.shape[:-1] + (-1, 32))
    amax = np.abs(blocks).max(-1, keepdims=True)
    byte = np.maximum(np.where(amax > 0, np.frexp(amax)[1] - 1 + 127, 0) - down, 1)
    scale = np.exp2(byte - 127.0)
    codes = (blocks / scale).astype(np.float32).astype(dtype).astype(np.float64)
    return np.moveaxis((codes * scale).reshape(v.shape), -1, axis)


WIDE = False


def mx_kscale(k):
    if not WIDE:
        return np.ones(k)
    levels = np.array([10, -10, 5, -5, 0])
    a = np.random.permutation(np.resize(levels, k // 512 * 4)).reshape(k // 512, 4)
    idx = np.arange(k)
    return np.exp2(a[idx // 512, idx % 128 // 32])


BF16 = ml_dtypes.bfloat16


def bf(x):
    return np.asarray(x, np.float32).astype(BF16)


def f64(x):
    return np.asarray(x).astype(np.float64)


E2M1 = np.array([0.0, 0.5, 1.0, 1.5, 2.0, 3.0, 4.0, 6.0, -0.0, -0.5, -1.0, -1.5, -2.0, -3.0, -4.0, -6.0])


def pack_weight(w, fmt):
    k, n = w.shape
    w = f64(bf(w)).reshape(k // 32, 32, n)
    amax = np.abs(w).max(1)
    if fmt == "e4m3":
        byte = np.frexp(amax)[1] - 1 + 127 - 7
    else:
        mant, ex = np.frexp(amax / 6.0)
        byte = np.where(mant > 0.5, ex, ex - 1) + 127
    byte = np.clip(np.where(amax > 0, byte, 1), 1, 254)
    scaled = (w * np.exp2(127.0 - byte)[:, None, :]).reshape(k, n).astype(np.float32)
    by_word = np.ascontiguousarray(scaled.reshape(k // 512, 128, 4, n).transpose(0, 1, 3, 2))
    if fmt == "e4m3":
        words = by_word.astype(ml_dtypes.float8_e4m3fn).view(np.uint8)
    else:
        c = by_word.astype(ml_dtypes.float4_e2m1fn).view(np.uint8) & 0xF
        words = c[..., 0::2] | (c[..., 1::2] << 4)
    return np.ascontiguousarray(words), np.ascontiguousarray(byte.astype(np.uint8).reshape(k // 512, 16, n))


def unpack_weight(words, scales, fmt):
    g, p, n, _ = words.shape
    if fmt == "e4m3":
        vals = np.ascontiguousarray(words).view(ml_dtypes.float8_e4m3fn).astype(np.float64)
    else:
        nib = np.empty((g, p, n, 4), np.uint8)
        nib[..., 0::2] = words & 0xF
        nib[..., 1::2] = words >> 4
        vals = E2M1[nib]
    vals = vals * np.repeat(np.exp2(scales.astype(np.float64) - 127.0), 8, axis=1)[..., None]
    return vals.transpose(0, 1, 3, 2).reshape(g * 512, n)


B, P, D = 128, 2, 3072
IN = P * D


def sigmoid(v):
    return 1.0 / (1.0 + np.exp(-v))


def setup_inputs():
    s = mx_kscale(D)
    sf = np.tile(s, P)
    x = bf(np.random.standard_normal((B, IN)) * sf)
    stack = np.random.standard_normal((P, D, D)) / np.sqrt(D) / s[None, :, None] * s[None, None, :]
    words, scales = pack_weight(stack.reshape(-1, D), "e4m3")
    return {"x": x,
            "weights_words": words,
            "weights_scales": scales,
            "bias": bf(np.random.standard_normal(IN) * 0.3 * sf),
            "gain": bf(1.3 + 0.1 * np.random.standard_normal(1)),
            "norm_bias": bf((0.3 + 0.05 * np.random.standard_normal(1)) * s.min()),
            "gamma": bf(0.5 + 0.3 * np.random.standard_normal(IN)),
            "beta": bf(np.random.standard_normal(IN) / sf)}


def reference(x, weights_words, weights_scales, bias, gain, norm_bias, gamma, beta):
    x, gamma = f64(x), f64(gamma)
    x_norm = x * f64(gain) + f64(norm_bias)
    xp = x_norm.reshape(B, P, D)
    yp = mxq(xp, 2, "e4m3").transpose(1, 0, 2) @ unpack_weight(weights_words, weights_scales, "e4m3").reshape(P, D, D)
    y = yp.transpose(1, 0, 2).reshape(B, IN) + f64(bias)
    mult = gamma + sigmoid(f64(beta) * y) * (1.0 - gamma)
    o = mult * y
    return o + x

@@ -1,0 +1,208 @@
+import concourse.mybir as mybir
+from concourse.masks import make_identity
+
+F32 = mybir.dt.float32
+BF16 = mybir.dt.bfloat16
+I32 = mybir.dt.int32
+U32 = mybir.dt.uint32
+U8 = mybir.dt.uint8
+FP8X4 = mybir.dt.float8_e4m3fn_x4
+ALU = mybir.AluOpType
+ACT = mybir.ActivationFunctionType
+
+P = 128
+PARTS = 2
+D = 3072
+FEATURES = PARTS * D
+K_PASS = 512
+GROUPS_PER_PART = D // K_PASS
+GROUPS = PARTS * GROUPS_PER_PART
+WORDS_PER_GROUP = K_PASS // 2
+N_TILE = 128
+N_TILES = FEATURES // N_TILE
+BANK_TILES = 4
+BANK_COLS = BANK_TILES * N_TILE
+CHUNK_COLS = 1024
+CHUNK_BANKS = CHUNK_COLS // BANK_COLS
+CHUNKS_PER_PART = D // CHUNK_COLS
+CHUNKS = PARTS * CHUNKS_PER_PART
+PLANES_PER_SET = 4
+PLANE_SETS = GROUPS // PLANES_PER_SET
+
+FLOPS = 2 * P * D * D * PARTS
+
+
+def tile_better_transformer_w_e_kernel(
+    tc, x, weights_words, weights_scales, bias, gain, norm_bias, gamma, beta, out
+):
+    nc = tc.nc
+    w_words = weights_words.rearrange("g p n t -> g p (n t)").bitcast(I32)
+    w_scales = weights_scales.bitcast(I32)
+
+    with tc.tile_pool(name="keep", bufs=1) as keep, tc.tile_pool(
+        name="weights", bufs=CHUNKS
+    ) as weights, tc.tile_pool(name="results", bufs=CHUNKS) as results, tc.tile_pool(
+        name="stage", bufs=2
+    ) as stage, tc.tile_pool(name="work", bufs=3) as work, tc.psum_pool(
+        name="psum_x", bufs=2
+    ) as psum_x, tc.psum_pool(name="psum_acc", bufs=4) as psum_acc, tc.psum_pool(
+        name="psum_back", bufs=2
+    ) as psum_back:
+        x_sb = keep.tile([P, FEATURES], BF16)
+        for e in range(PARTS):
+            nc.sync.dma_start(out=x_sb[:, e * D : (e + 1) * D], in_=x[:, e * D : (e + 1) * D])
+
+        planes = keep.tile([P, PLANE_SETS, D], U8, align_bytes=64)
+        nc.vector.memset(planes[:].bitcast(I32), 0)
+        for s in range(PLANE_SETS):
+            for q in range(4):
+                nc.sync.dma_start(
+                    out=planes[32 * q : 32 * q + 16, s, :].bitcast(I32),
+                    in_=w_scales[PLANES_PER_SET * s : PLANES_PER_SET * (s + 1), 4 * q : 4 * q + 4, :],
+                )
+
+        w_chunks = []
+        for e in range(PARTS):
+            for c in range(CHUNKS_PER_PART):
+                w_sb = weights.tile([P, GROUPS_PER_PART, CHUNK_COLS], I32, align_bytes=64)
+                nc.sync.dma_start(
+                    out=w_sb[:],
+                    in_=w_words[
+                        e * GROUPS_PER_PART : (e + 1) * GROUPS_PER_PART,
+                        :,
+                        c * CHUNK_COLS : (c + 1) * CHUNK_COLS,
+                    ].rearrange("g p n -> p g n"),
+                )
+                w_chunks.append(w_sb)
+
+        gain_bf = keep.tile([P, 1], BF16)
+        nc.scalar.dma_start(out=gain_bf[:], in_=gain.partition_broadcast(P))
+        shift_bf = keep.tile([P, 1], BF16)
+        nc.scalar.dma_start(out=shift_bf[:], in_=norm_bias.partition_broadcast(P))
+        vec_rows = keep.tile([P, 3, P], BF16)
+        nc.vector.memset(vec_rows[:], 0.0)
+        for v, vec in enumerate((bias, gamma, beta)):
+            nc.scalar.dma_start(
+                out=vec_rows[0:N_TILES, v, :], in_=vec.rearrange("(j p) -> j p", p=P)
+            )
+
+        ident_f32 = keep.tile([P, P], F32)
+        make_identity(nc, ident_f32[:])
+        ident_bf = keep.tile([P, P], BF16)
+        nc.vector.tensor_copy(out=ident_bf[:], in_=ident_f32[:])
+        gain_f32 = keep.tile([P, 1], F32)
+        nc.vector.tensor_copy(out=gain_f32[:], in_=gain_bf[:])
+        shift_f32 = keep.tile([P, 1], F32)
+        nc.vector.tensor_copy(out=shift_f32[:], in_=shift_bf[:])
+
+        x_words = x_sb[:].bitcast(F32)
+        x_codes = keep.tile([P, GROUPS * P], U32, align_bytes=64)
+        x_scales = keep.tile([P, GROUPS * P], U8, align_bytes=64)
+        for pair in range(GROUPS // 2):
+            xt = psum_x.tile([P, 2, 2, P], F32, tag="xt")
+            for i in range(2):
+                g = 2 * pair + i
+                for u in range(2):
+                    nc.tensor.transpose(
+                        xt[:, i, u, :],
+                        x_words[:, WORDS_PER_GROUP * g + u : WORDS_PER_GROUP * (g + 1) : 2],
+                        ident_f32[:],
+                    )
+            grouped = stage.tile([P, 2, K_PASS], BF16, align_bytes=64)
+            for i in range(2):
+                nc.scalar.activation(
+                    out=grouped[:, i, :].rearrange("p (b u e) -> p b u e", u=2, e=2),
+                    in_=xt[:, i, :, :].bitcast(BF16).rearrange("p u (b e) -> p b u e", e=2),
+                    func=ACT.Identity,
+                    scale=gain_f32[:, 0:1],
+                    bias=shift_f32[:, 0:1],
+                )
+            nc.vector.quantize_mx(
+                out=x_codes[:, 2 * P * pair : 2 * P * (pair + 1)].bitcast(FP8X4),
+                scales=x_scales[:, 2 * P * pair : 2 * P * (pair + 1)],
+                in_=grouped[:].rearrange("p i c -> p (i c)"),
+            )
+
+        vec_t = psum_x.tile([P, 3, P], BF16, tag="xt")
+        for v in range(3):
+            nc.tensor.transpose(vec_t[:, v, :], vec_rows[:, v, :], ident_bf[:])
+        vec_cols = keep.tile([P, 3, N_TILES], F32)
+        nc.vector.tensor_copy(out=vec_cols[:], in_=vec_t[:, :, 0:N_TILES])
+        bias_col = vec_cols[:, 0, :]
+        gamma_col = vec_cols[:, 1, :]
+        beta_col = vec_cols[:, 2, :]
+        rest_col = keep.tile([P, N_TILES], F32)
+        nc.vector.tensor_scalar(
+            out=rest_col[:], in0=gamma_col, scalar1=-1.0, scalar2=1.0, op0=ALU.mult, op1=ALU.add
+        )
+
+        for e in range(PARTS):
+            for c in range(CHUNKS_PER_PART):
+                w_sb = w_chunks[e * CHUNKS_PER_PART + c]
+                accs = []
+                for h in range(CHUNK_BANKS):
+                    acc = psum_acc.tile([P, BANK_TILES, P], F32)
+                    for j in range(BANK_TILES):
+                        n0 = h * BANK_COLS + j * N_TILE
+                        d0 = c * CHUNK_COLS + n0
+                        for i in range(GROUPS_PER_PART):
+                            g = e * GROUPS_PER_PART + i
+                            nc.tensor.matmul_mx(
+                                out=acc[:, j, :],
+                                lhsT=w_sb[:, i, n0 : n0 + N_TILE].bitcast(FP8X4),
+                                lhsT_scale=planes[
+                                    4 * (g % PLANES_PER_SET) : P, g // PLANES_PER_SET, d0 : d0 + N_TILE
+                                ],
+                                rhs=x_codes[:, g * P : (g + 1) * P].bitcast(FP8X4),
+                                rhs_scale=x_scales[:, g * P : (g + 1) * P],
+                                start=(i == 0),
+                                stop=(i == GROUPS_PER_PART - 1),
+                            )
+                    accs.append(acc)
+
+                products = []
+                for h in range(CHUNK_BANKS):
+                    t0 = (e * D + c * CHUNK_COLS + h * BANK_COLS) // N_TILE
+                    y = work.tile([P, BANK_TILES, P], F32)
+                    nc.vector.tensor_tensor(
+                        out=y[:],
+                        in0=accs[h][:],
+                        in1=bias_col[:, t0 : t0 + BANK_TILES].unsqueeze(2).to_broadcast([P, BANK_TILES, P]),
+                        op=ALU.add,
+                    )
+                    mult = work.tile([P, BANK_TILES, P], F32)
+                    for j in range(BANK_TILES):
+                        nc.scalar.activation(
+                            out=mult[:, j, :],
+                            in_=y[:, j, :],
+                            func=ACT.Sigmoid,
+                            scale=beta_col[:, t0 + j : t0 + j + 1],
+                        )
+                    for j in range(BANK_TILES):
+                        nc.vector.tensor_scalar(
+                            out=mult[:, j, :],
+                            in0=mult[:, j, :],
+                            scalar1=rest_col[:, t0 + j : t0 + j + 1],
+                            scalar2=gamma_col[:, t0 + j : t0 + j + 1],
+                            op0=ALU.mult,
+                            op1=ALU.add,
+                        )
+                    product = work.tile([P, BANK_TILES, P], F32)
+                    nc.vector.tensor_tensor(out=product[:], in0=mult[:], in1=y[:], op=ALU.mult)
+                    products.append(product)
+
+                f0 = e * D + c * CHUNK_COLS
+                out_sb = results.tile([P, CHUNK_COLS], F32)
+                for h in range(CHUNK_BANKS):
+                    back = psum_back.tile([P, BANK_COLS], F32)
+                    for j in range(BANK_TILES):
+                        nc.tensor.transpose(
+                            back[:, j * N_TILE : (j + 1) * N_TILE], products[h][:, j, :], ident_f32[:]
+                        )
+                    nc.vector.tensor_tensor(
+                        out=out_sb[:, h * BANK_COLS : (h + 1) * BANK_COLS],
+                        in0=back[:],
+                        in1=x_sb[:, f0 + h * BANK_COLS : f0 + (h + 1) * BANK_COLS],
+                        op=ALU.add,
+                    )
+                nc.sync.dma_start(out=out[:, f0 : f0 + CHUNK_COLS], in_=out_sb[:])

@@ -20,12 +20,12 @@ GROUPS = PARTS * GROUPS_PER_PART
 WORDS_PER_GROUP = K_PASS // 2
 N_TILE = 128
 N_TILES = FEATURES // N_TILE
-BANK_TILES = 4
-BANK_COLS = BANK_TILES * N_TILE
-CHUNK_COLS = 1024
-CHUNK_BANKS = CHUNK_COLS // BANK_COLS
-CHUNKS_PER_PART = D // CHUNK_COLS
-CHUNKS = PARTS * CHUNKS_PER_PART
+UNIT_TILES = 4
+UNIT_COLS = UNIT_TILES * N_TILE
+UNITS_PER_PART = D // UNIT_COLS
+UNITS = PARTS * UNITS_PER_PART
+LOAD_UNITS = 2
+TAPER_UNITS = 0
 PLANES_PER_SET = 4
 PLANE_SETS = GROUPS // PLANES_PER_SET
 
@@ -39,41 +39,41 @@ def tile_better_transformer_w_e_kernel(
     w_words = weights_words.rearrange("g p n t -> g p (n t)").bitcast(I32)
     w_scales = weights_scales.bitcast(I32)
 
-    with tc.tile_pool(name="keep", bufs=1) as keep, tc.tile_pool(
-        name="weights", bufs=CHUNKS
-    ) as weights, tc.tile_pool(name="results", bufs=CHUNKS) as results, tc.tile_pool(
-        name="stage", bufs=2
-    ) as stage, tc.tile_pool(name="work", bufs=3) as work, tc.psum_pool(
-        name="psum_x", bufs=2
-    ) as psum_x, tc.psum_pool(name="psum_acc", bufs=4) as psum_acc, tc.psum_pool(
-        name="psum_back", bufs=2
-    ) as psum_back:
+    batches = [(k, LOAD_UNITS) for k in range(0, UNITS - TAPER_UNITS, LOAD_UNITS)]
+    batches.extend((k, 1) for k in range(UNITS - TAPER_UNITS, UNITS))
+
+    with tc.tile_pool(name="keep", bufs=1) as keep, tc.tile_pool(name="stage", bufs=2) as stage, tc.tile_pool(
+        name="work", bufs=3
+    ) as work, tc.psum_pool(name="psum_x", bufs=2) as psum_x, tc.psum_pool(
+        name="psum_acc", bufs=4
+    ) as psum_acc, tc.psum_pool(name="psum_back", bufs=2) as psum_back, tc.manual_schedule():
+        planes = keep.tile([P, PLANE_SETS, D], U8, align_bytes=64)
+        nc.vector.memset(planes[:].bitcast(I32), 0)
         x_sb = keep.tile([P, FEATURES], BF16)
         for e in range(PARTS):
             nc.sync.dma_start(out=x_sb[:, e * D : (e + 1) * D], in_=x[:, e * D : (e + 1) * D])
-
-        planes = keep.tile([P, PLANE_SETS, D], U8, align_bytes=64)
-        nc.vector.memset(planes[:].bitcast(I32), 0)
         for s in range(PLANE_SETS):
             for q in range(4):
                 nc.sync.dma_start(
                     out=planes[32 * q : 32 * q + 16, s, :].bitcast(I32),
                     in_=w_scales[PLANES_PER_SET * s : PLANES_PER_SET * (s + 1), 4 * q : 4 * q + 4, :],
                 )
-
-        w_chunks = []
-        for e in range(PARTS):
-            for c in range(CHUNKS_PER_PART):
-                w_sb = weights.tile([P, GROUPS_PER_PART, CHUNK_COLS], I32, align_bytes=64)
-                nc.sync.dma_start(
-                    out=w_sb[:],
-                    in_=w_words[
-                        e * GROUPS_PER_PART : (e + 1) * GROUPS_PER_PART,
-                        :,
-                        c * CHUNK_COLS : (c + 1) * CHUNK_COLS,
-                    ].rearrange("g p n -> p g n"),
-                )
-                w_chunks.append(w_sb)
+        w_of = {}
+        out_of = {}
+        for first, count in batches:
+            e = first // UNITS_PER_PART
+            d0 = (first % UNITS_PER_PART) * UNIT_COLS
+            w_sb = keep.tile([P, GROUPS_PER_PART, count * UNIT_COLS], I32, name="w%d" % first, align_bytes=64)
+            nc.sync.dma_start(
+                out=w_sb[:],
+                in_=w_words[
+                    e * GROUPS_PER_PART : (e + 1) * GROUPS_PER_PART, :, d0 : d0 + count * UNIT_COLS
+                ].rearrange("g p n -> p g n"),
+            )
+            out_sb = keep.tile([P, count * UNIT_COLS], F32, name="out%d" % first)
+            for k in range(first, first + count):
+                w_of[k] = (w_sb, (k - first) * UNIT_COLS)
+                out_of[k] = (out_sb, (k - first) * UNIT_COLS)
 
         gain_bf = keep.tile([P, 1], BF16)
         nc.scalar.dma_start(out=gain_bf[:], in_=gain.partition_broadcast(P))
@@ -82,9 +82,7 @@ def tile_better_transformer_w_e_kernel(
         vec_rows = keep.tile([P, 3, P], BF16)
         nc.vector.memset(vec_rows[:], 0.0)
         for v, vec in enumerate((bias, gamma, beta)):
-            nc.scalar.dma_start(
-                out=vec_rows[0:N_TILES, v, :], in_=vec.rearrange("(j p) -> j p", p=P)
-            )
+            nc.scalar.dma_start(out=vec_rows[0:N_TILES, v, :], in_=vec.rearrange("(j p) -> j p", p=P))
 
         ident_f32 = keep.tile([P, P], F32)
         make_identity(nc, ident_f32[:])
@@ -136,73 +134,84 @@ def tile_better_transformer_w_e_kernel(
             out=rest_col[:], in0=gamma_col, scalar1=-1.0, scalar2=1.0, op0=ALU.mult, op1=ALU.add
         )
 
-        for e in range(PARTS):
-            for c in range(CHUNKS_PER_PART):
-                w_sb = w_chunks[e * CHUNKS_PER_PART + c]
-                accs = []
-                for h in range(CHUNK_BANKS):
-                    acc = psum_acc.tile([P, BANK_TILES, P], F32)
-                    for j in range(BANK_TILES):
-                        n0 = h * BANK_COLS + j * N_TILE
-                        d0 = c * CHUNK_COLS + n0
-                        for i in range(GROUPS_PER_PART):
-                            g = e * GROUPS_PER_PART + i
-                            nc.tensor.matmul_mx(
-                                out=acc[:, j, :],
-                                lhsT=w_sb[:, i, n0 : n0 + N_TILE].bitcast(FP8X4),
-                                lhsT_scale=planes[
-                                    4 * (g % PLANES_PER_SET) : P, g // PLANES_PER_SET, d0 : d0 + N_TILE
-                                ],
-                                rhs=x_codes[:, g * P : (g + 1) * P].bitcast(FP8X4),
-                                rhs_scale=x_scales[:, g * P : (g + 1) * P],
-                                start=(i == 0),
-                                stop=(i == GROUPS_PER_PART - 1),
-                            )
-                    accs.append(acc)
+        acc_of = {}
+        y_of = {}
+        mult_of = {}
+        product_of = {}
 
-                products = []
-                for h in range(CHUNK_BANKS):
-                    t0 = (e * D + c * CHUNK_COLS + h * BANK_COLS) // N_TILE
-                    y = work.tile([P, BANK_TILES, P], F32)
-                    nc.vector.tensor_tensor(
-                        out=y[:],
-                        in0=accs[h][:],
-                        in1=bias_col[:, t0 : t0 + BANK_TILES].unsqueeze(2).to_broadcast([P, BANK_TILES, P]),
-                        op=ALU.add,
+        def multiply(k):
+            w_sb, n_first = w_of[k]
+            e = k // UNITS_PER_PART
+            acc = psum_acc.tile([P, UNIT_TILES, P], F32)
+            for j in range(UNIT_TILES):
+                n0 = n_first + j * N_TILE
+                d0 = (k % UNITS_PER_PART) * UNIT_COLS + j * N_TILE
+                for i in range(GROUPS_PER_PART):
+                    g = e * GROUPS_PER_PART + i
+                    nc.tensor.matmul_mx(
+                        out=acc[:, j, :],
+                        lhsT=w_sb[:, i, n0 : n0 + N_TILE].bitcast(FP8X4),
+                        lhsT_scale=planes[4 * (g % PLANES_PER_SET) : P, g // PLANES_PER_SET, d0 : d0 + N_TILE],
+                        rhs=x_codes[:, g * P : (g + 1) * P].bitcast(FP8X4),
+                        rhs_scale=x_scales[:, g * P : (g + 1) * P],
+                        start=(i == 0),
+                        stop=(i == GROUPS_PER_PART - 1),
                     )
-                    mult = work.tile([P, BANK_TILES, P], F32)
-                    for j in range(BANK_TILES):
-                        nc.scalar.activation(
-                            out=mult[:, j, :],
-                            in_=y[:, j, :],
-                            func=ACT.Sigmoid,
-                            scale=beta_col[:, t0 + j : t0 + j + 1],
-                        )
-                    for j in range(BANK_TILES):
-                        nc.vector.tensor_scalar(
-                            out=mult[:, j, :],
-                            in0=mult[:, j, :],
-                            scalar1=rest_col[:, t0 + j : t0 + j + 1],
-                            scalar2=gamma_col[:, t0 + j : t0 + j + 1],
-                            op0=ALU.mult,
-                            op1=ALU.add,
-                        )
-                    product = work.tile([P, BANK_TILES, P], F32)
-                    nc.vector.tensor_tensor(out=product[:], in0=mult[:], in1=y[:], op=ALU.mult)
-                    products.append(product)
+            acc_of[k] = acc
 
-                f0 = e * D + c * CHUNK_COLS
-                out_sb = results.tile([P, CHUNK_COLS], F32)
-                for h in range(CHUNK_BANKS):
-                    back = psum_back.tile([P, BANK_COLS], F32)
-                    for j in range(BANK_TILES):
-                        nc.tensor.transpose(
-                            back[:, j * N_TILE : (j + 1) * N_TILE], products[h][:, j, :], ident_f32[:]
-                        )
-                    nc.vector.tensor_tensor(
-                        out=out_sb[:, h * BANK_COLS : (h + 1) * BANK_COLS],
-                        in0=back[:],
-                        in1=x_sb[:, f0 + h * BANK_COLS : f0 + (h + 1) * BANK_COLS],
-                        op=ALU.add,
-                    )
-                nc.sync.dma_start(out=out[:, f0 : f0 + CHUNK_COLS], in_=out_sb[:])
+        def squash(k):
+            t0 = k * UNIT_TILES
+            y = work.tile([P, UNIT_TILES, P], F32)
+            nc.vector.tensor_tensor(
+                out=y[:],
+                in0=acc_of[k][:],
+                in1=bias_col[:, t0 : t0 + UNIT_TILES].unsqueeze(2).to_broadcast([P, UNIT_TILES, P]),
+                op=ALU.add,
+            )
+            mult = work.tile([P, UNIT_TILES, P], F32)
+            for j in range(UNIT_TILES):
+                nc.scalar.activation(
+                    out=mult[:, j, :], in_=y[:, j, :], func=ACT.Sigmoid, scale=beta_col[:, t0 + j : t0 + j + 1]
+                )
+            y_of[k] = y
+            mult_of[k] = mult
+
+        def gate(k):
+            t0 = k * UNIT_TILES
+            mult = mult_of[k]
+            for j in range(UNIT_TILES):
+                nc.vector.tensor_scalar(
+                    out=mult[:, j, :],
+                    in0=mult[:, j, :],
+                    scalar1=rest_col[:, t0 + j : t0 + j + 1],
+                    scalar2=gamma_col[:, t0 + j : t0 + j + 1],
+                    op0=ALU.mult,
+                    op1=ALU.add,
+                )
+            product = work.tile([P, UNIT_TILES, P], F32)
+            nc.vector.tensor_tensor(out=product[:], in0=mult[:], in1=y_of[k][:], op=ALU.mult)
+            product_of[k] = product
+
+        def finish(k):
+            back = psum_back.tile([P, UNIT_COLS], F32)
+            for j in range(UNIT_TILES):
+                nc.tensor.transpose(back[:, j * N_TILE : (j + 1) * N_TILE], product_of[k][:, j, :], ident_f32[:])
+            out_sb, c0 = out_of[k]
+            nc.vector.tensor_tensor(
+                out=out_sb[:, c0 : c0 + UNIT_COLS],
+                in0=back[:],
+                in1=x_sb[:, k * UNIT_COLS : (k + 1) * UNIT_COLS],
+                op=ALU.add,
+            )
+            if c0 + UNIT_COLS == out_sb.shape[1]:
+                nc.sync.dma_start(out=out[:, (k + 1) * UNIT_COLS - out_sb.shape[1] : (k + 1) * UNIT_COLS], in_=out_sb[:])
+
+        for step in range(UNITS + 2):
+            if step < UNITS:
+                multiply(step)
+            if 1 <= step <= UNITS:
+                gate(step - 1)
+            if step < UNITS:
+                squash(step)
+            if step >= 2:
+                finish(step - 2)

@@ -20,16 +20,21 @@ GROUPS = PARTS * GROUPS_PER_PART
 WORDS_PER_GROUP = K_PASS // 2
 N_TILE = 128
 N_TILES = FEATURES // N_TILE
+TILES_PER_PART = D // N_TILE
 UNIT_TILES = 4
-UNIT_COLS = UNIT_TILES * N_TILE
-UNITS_PER_PART = D // UNIT_COLS
-UNITS = PARTS * UNITS_PER_PART
-LOAD_UNITS = 2
-TAPER_UNITS = 0
+LOAD_TILES = 8
 PLANES_PER_SET = 4
 PLANE_SETS = GROUPS // PLANES_PER_SET
 
 FLOPS = 2 * P * D * D * PARTS
+
+
+def halve_last(sizes):
+    return sizes[:-1] + [sizes[-1] // 2, sizes[-1] // 2]
+
+
+def starts_and_sizes(sizes):
+    return [(sum(sizes[:i]), size) for i, size in enumerate(sizes)]
 
 
 def tile_better_transformer_w_e_kernel(
@@ -39,8 +44,8 @@ def tile_better_transformer_w_e_kernel(
     w_words = weights_words.rearrange("g p n t -> g p (n t)").bitcast(I32)
     w_scales = weights_scales.bitcast(I32)
 
-    batches = [(k, LOAD_UNITS) for k in range(0, UNITS - TAPER_UNITS, LOAD_UNITS)]
-    batches.extend((k, 1) for k in range(UNITS - TAPER_UNITS, UNITS))
+    loads = starts_and_sizes(halve_last([LOAD_TILES] * (N_TILES // LOAD_TILES)))
+    units = starts_and_sizes(halve_last([UNIT_TILES] * (N_TILES // UNIT_TILES)))
 
     with tc.tile_pool(name="keep", bufs=1) as keep, tc.tile_pool(name="stage", bufs=2) as stage, tc.tile_pool(
         name="work", bufs=3
@@ -60,20 +65,20 @@ def tile_better_transformer_w_e_kernel(
                 )
         w_of = {}
         out_of = {}
-        for first, count in batches:
-            e = first // UNITS_PER_PART
-            d0 = (first % UNITS_PER_PART) * UNIT_COLS
-            w_sb = keep.tile([P, GROUPS_PER_PART, count * UNIT_COLS], I32, name="w%d" % first, align_bytes=64)
+        for first, count in loads:
+            e = first // TILES_PER_PART
+            d0 = (first % TILES_PER_PART) * N_TILE
+            w_sb = keep.tile([P, GROUPS_PER_PART, count * N_TILE], I32, name="w%d" % first, align_bytes=64)
             nc.sync.dma_start(
                 out=w_sb[:],
                 in_=w_words[
-                    e * GROUPS_PER_PART : (e + 1) * GROUPS_PER_PART, :, d0 : d0 + count * UNIT_COLS
+                    e * GROUPS_PER_PART : (e + 1) * GROUPS_PER_PART, :, d0 : d0 + count * N_TILE
                 ].rearrange("g p n -> p g n"),
             )
-            out_sb = keep.tile([P, count * UNIT_COLS], F32, name="out%d" % first)
-            for k in range(first, first + count):
-                w_of[k] = (w_sb, (k - first) * UNIT_COLS)
-                out_of[k] = (out_sb, (k - first) * UNIT_COLS)
+            out_sb = keep.tile([P, count * N_TILE], F32, name="out%d" % first)
+            for t in range(first, first + count):
+                w_of[t] = (w_sb, (t - first) * N_TILE)
+                out_of[t] = (out_sb, (t - first) * N_TILE)
 
         gain_bf = keep.tile([P, 1], BF16)
         nc.scalar.dma_start(out=gain_bf[:], in_=gain.partition_broadcast(P))
@@ -140,14 +145,14 @@ def tile_better_transformer_w_e_kernel(
         product_of = {}
 
         def multiply(k):
-            w_sb, n_first = w_of[k]
-            e = k // UNITS_PER_PART
-            acc = psum_acc.tile([P, UNIT_TILES, P], F32)
-            for j in range(UNIT_TILES):
-                n0 = n_first + j * N_TILE
-                d0 = (k % UNITS_PER_PART) * UNIT_COLS + j * N_TILE
+            first, count = units[k]
+            acc = psum_acc.tile([P, count, P], F32)
+            for j in range(count):
+                t = first + j
+                w_sb, n0 = w_of[t]
+                d0 = (t % TILES_PER_PART) * N_TILE
                 for i in range(GROUPS_PER_PART):
-                    g = e * GROUPS_PER_PART + i
+                    g = (t // TILES_PER_PART) * GROUPS_PER_PART + i
                     nc.tensor.matmul_mx(
                         out=acc[:, j, :],
                         lhsT=w_sb[:, i, n0 : n0 + N_TILE].bitcast(FP8X4),
@@ -160,58 +165,58 @@ def tile_better_transformer_w_e_kernel(
             acc_of[k] = acc
 
         def squash(k):
-            t0 = k * UNIT_TILES
-            y = work.tile([P, UNIT_TILES, P], F32)
+            first, count = units[k]
+            y = work.tile([P, count, P], F32)
             nc.vector.tensor_tensor(
                 out=y[:],
                 in0=acc_of[k][:],
-                in1=bias_col[:, t0 : t0 + UNIT_TILES].unsqueeze(2).to_broadcast([P, UNIT_TILES, P]),
+                in1=bias_col[:, first : first + count].unsqueeze(2).to_broadcast([P, count, P]),
                 op=ALU.add,
             )
-            mult = work.tile([P, UNIT_TILES, P], F32)
-            for j in range(UNIT_TILES):
+            mult = work.tile([P, count, P], F32)
+            for j in range(count):
                 nc.scalar.activation(
-                    out=mult[:, j, :], in_=y[:, j, :], func=ACT.Sigmoid, scale=beta_col[:, t0 + j : t0 + j + 1]
+                    out=mult[:, j, :], in_=y[:, j, :], func=ACT.Sigmoid, scale=beta_col[:, first + j : first + j + 1]
                 )
             y_of[k] = y
             mult_of[k] = mult
 
         def gate(k):
-            t0 = k * UNIT_TILES
+            first, count = units[k]
             mult = mult_of[k]
-            for j in range(UNIT_TILES):
+            for j in range(count):
                 nc.vector.tensor_scalar(
                     out=mult[:, j, :],
                     in0=mult[:, j, :],
-                    scalar1=rest_col[:, t0 + j : t0 + j + 1],
-                    scalar2=gamma_col[:, t0 + j : t0 + j + 1],
+                    scalar1=rest_col[:, first + j : first + j + 1],
+                    scalar2=gamma_col[:, first + j : first + j + 1],
                     op0=ALU.mult,
                     op1=ALU.add,
                 )
-            product = work.tile([P, UNIT_TILES, P], F32)
+            product = work.tile([P, count, P], F32)
             nc.vector.tensor_tensor(out=product[:], in0=mult[:], in1=y_of[k][:], op=ALU.mult)
             product_of[k] = product
 
         def finish(k):
-            back = psum_back.tile([P, UNIT_COLS], F32)
-            for j in range(UNIT_TILES):
+            first, count = units[k]
+            back = psum_back.tile([P, count * N_TILE], F32)
+            for j in range(count):
                 nc.tensor.transpose(back[:, j * N_TILE : (j + 1) * N_TILE], product_of[k][:, j, :], ident_f32[:])
-            out_sb, c0 = out_of[k]
+            out_sb, c0 = out_of[first]
+            c1 = c0 + count * N_TILE
+            f1 = (first + count) * N_TILE
             nc.vector.tensor_tensor(
-                out=out_sb[:, c0 : c0 + UNIT_COLS],
-                in0=back[:],
-                in1=x_sb[:, k * UNIT_COLS : (k + 1) * UNIT_COLS],
-                op=ALU.add,
+                out=out_sb[:, c0:c1], in0=back[:], in1=x_sb[:, first * N_TILE : f1], op=ALU.add
             )
-            if c0 + UNIT_COLS == out_sb.shape[1]:
-                nc.sync.dma_start(out=out[:, (k + 1) * UNIT_COLS - out_sb.shape[1] : (k + 1) * UNIT_COLS], in_=out_sb[:])
+            if c1 == out_sb.shape[1]:
+                nc.sync.dma_start(out=out[:, f1 - c1 : f1], in_=out_sb[:])
 
-        for step in range(UNITS + 2):
-            if step < UNITS:
+        for step in range(len(units) + 2):
+            if step < len(units):
                 multiply(step)
-            if 1 <= step <= UNITS:
+            if 1 <= step <= len(units):
                 gate(step - 1)
-            if step < UNITS:
+            if step < len(units):
                 squash(step)
             if step >= 2:
                 finish(step - 2)

@@ -139,8 +139,10 @@ def tile_better_transformer_w_e_kernel(
             out=rest_col[:], in0=gamma_col, scalar1=-1.0, scalar2=1.0, op0=ALU.mult, op1=ALU.add
         )
 
+        beta_bias_col = keep.tile([P, N_TILES], F32)
+        nc.vector.tensor_tensor(out=beta_bias_col[:], in0=beta_col, in1=bias_col, op=ALU.mult)
+
         acc_of = {}
-        y_of = {}
         mult_of = {}
         product_of = {}
 
@@ -166,35 +168,42 @@ def tile_better_transformer_w_e_kernel(
 
         def squash(k):
             first, count = units[k]
-            y = work.tile([P, count, P], F32)
-            nc.vector.tensor_tensor(
-                out=y[:],
-                in0=acc_of[k][:],
-                in1=bias_col[:, first : first + count].unsqueeze(2).to_broadcast([P, count, P]),
-                op=ALU.add,
-            )
             mult = work.tile([P, count, P], F32)
             for j in range(count):
+                t = first + j
                 nc.scalar.activation(
-                    out=mult[:, j, :], in_=y[:, j, :], func=ACT.Sigmoid, scale=beta_col[:, first + j : first + j + 1]
+                    out=mult[:, j, :],
+                    in_=acc_of[k][:, j, :],
+                    func=ACT.Sigmoid,
+                    scale=beta_col[:, t : t + 1],
+                    bias=beta_bias_col[:, t : t + 1],
                 )
-            y_of[k] = y
             mult_of[k] = mult
 
         def gate(k):
             first, count = units[k]
             mult = mult_of[k]
+            product = work.tile([P, count, P], F32)
             for j in range(count):
+                t = first + j
                 nc.vector.tensor_scalar(
                     out=mult[:, j, :],
                     in0=mult[:, j, :],
-                    scalar1=rest_col[:, first + j : first + j + 1],
-                    scalar2=gamma_col[:, first + j : first + j + 1],
+                    scalar1=rest_col[:, t : t + 1],
+                    scalar2=gamma_col[:, t : t + 1],
                     op0=ALU.mult,
                     op1=ALU.add,
                 )
-            product = work.tile([P, count, P], F32)
-            nc.vector.tensor_tensor(out=product[:], in0=mult[:], in1=y_of[k][:], op=ALU.mult)
+            for j in range(count):
+                t = first + j
+                nc.vector.scalar_tensor_tensor(
+                    out=product[:, j, :],
+                    in0=acc_of[k][:, j, :],
+                    scalar=bias_col[:, t : t + 1],
+                    in1=mult[:, j, :],
+                    op0=ALU.add,
+                    op1=ALU.mult,
+                )
             product_of[k] = product
 
         def finish(k):

@@ -22,15 +22,16 @@ N_TILE = 128
 N_TILES = FEATURES // N_TILE
 TILES_PER_PART = D // N_TILE
 UNIT_TILES = 4
-LOAD_TILES = 8
+LOADS = (8, 8, 8, 8, 4, 4, 4)
+LAST_TILES = 4
+UNITS = (UNIT_TILES,) * 11 + (2, 2)
+STORES = (32, 8, 4, 2, 2)
+FIRST_OF_LAST = N_TILES - LAST_TILES
+HALF = 3
 PLANES_PER_SET = 4
 PLANE_SETS = GROUPS // PLANES_PER_SET
 
 FLOPS = 2 * P * D * D * PARTS
-
-
-def halve_last(sizes):
-    return sizes[:-1] + [sizes[-1] // 2, sizes[-1] // 2]
 
 
 def starts_and_sizes(sizes):
@@ -42,42 +43,62 @@ def tile_better_transformer_w_e_kernel(
 ):
     nc = tc.nc
     w_words = weights_words.rearrange("g p n t -> g p (n t)").bitcast(I32)
-    w_scales = weights_scales.bitcast(I32)
+    w_scales = weights_scales
 
-    loads = starts_and_sizes(halve_last([LOAD_TILES] * (N_TILES // LOAD_TILES)))
-    units = starts_and_sizes(halve_last([UNIT_TILES] * (N_TILES // UNIT_TILES)))
+    loads = starts_and_sizes(LOADS)
+    units = starts_and_sizes(UNITS)
+    stores = starts_and_sizes(STORES)
 
     with tc.tile_pool(name="keep", bufs=1) as keep, tc.tile_pool(name="stage", bufs=2) as stage, tc.tile_pool(
         name="work", bufs=3
-    ) as work, tc.psum_pool(name="psum_x", bufs=2) as psum_x, tc.psum_pool(
-        name="psum_acc", bufs=4
-    ) as psum_acc, tc.psum_pool(name="psum_back", bufs=2) as psum_back, tc.manual_schedule():
+    ) as work, tc.psum_pool(name="psum", bufs=6) as psum, tc.psum_pool(
+        name="psum_back", bufs=2
+    ) as psum_back, tc.manual_schedule():
+        ident_f32 = keep.tile([P, P], F32)
+        make_identity(nc, ident_f32[:])
+
         planes = keep.tile([P, PLANE_SETS, D], U8, align_bytes=64)
-        nc.vector.memset(planes[:].bitcast(I32), 0)
+        for s in range(PLANE_SETS):
+            nc.vector.memset(planes[:, s, :].bitcast(I32), 0)
         x_sb = keep.tile([P, FEATURES], BF16)
         for e in range(PARTS):
             nc.sync.dma_start(out=x_sb[:, e * D : (e + 1) * D], in_=x[:, e * D : (e + 1) * D])
-        for s in range(PLANE_SETS):
+        for s in range(PLANE_SETS - 1):
             for q in range(4):
                 nc.sync.dma_start(
                     out=planes[32 * q : 32 * q + 16, s, :].bitcast(I32),
-                    in_=w_scales[PLANES_PER_SET * s : PLANES_PER_SET * (s + 1), 4 * q : 4 * q + 4, :],
+                    in_=w_scales[PLANES_PER_SET * s : PLANES_PER_SET * (s + 1), 4 * q : 4 * q + 4, :].bitcast(I32),
                 )
+        s = PLANE_SETS - 1
+        for q in range(4):
+            nc.gpsimd.dma_start(
+                out=planes[32 * q : 32 * q + 16, s, :].bitcast(F32),
+                in_=w_scales[PLANES_PER_SET * s : PLANES_PER_SET * (s + 1), 4 * q : 4 * q + 4, :].bitcast(F32),
+            )
         w_of = {}
-        out_of = {}
-        for first, count in loads:
+
+        def load_weights(first, count, i0, i1):
             e = first // TILES_PER_PART
             d0 = (first % TILES_PER_PART) * N_TILE
-            w_sb = keep.tile([P, GROUPS_PER_PART, count * N_TILE], I32, name="w%d" % first, align_bytes=64)
+            w_sb = keep.tile([P, i1 - i0, count * N_TILE], I32, name="w%d_%d" % (first, i0), align_bytes=64)
             nc.sync.dma_start(
                 out=w_sb[:],
                 in_=w_words[
-                    e * GROUPS_PER_PART : (e + 1) * GROUPS_PER_PART, :, d0 : d0 + count * N_TILE
+                    e * GROUPS_PER_PART + i0 : e * GROUPS_PER_PART + i1, :, d0 : d0 + count * N_TILE
                 ].rearrange("g p n -> p g n"),
             )
+            for j in range(count):
+                for i in range(i0, i1):
+                    w_of[first + j, i] = w_sb[:, i - i0, j * N_TILE : (j + 1) * N_TILE]
+
+        for first, count in loads:
+            load_weights(first, count, 0, GROUPS_PER_PART)
+        load_weights(FIRST_OF_LAST, LAST_TILES, 0, HALF)
+        load_weights(FIRST_OF_LAST, LAST_TILES, HALF, GROUPS_PER_PART)
+        out_of = {}
+        for first, count in stores:
             out_sb = keep.tile([P, count * N_TILE], F32, name="out%d" % first)
             for t in range(first, first + count):
-                w_of[t] = (w_sb, (t - first) * N_TILE)
                 out_of[t] = (out_sb, (t - first) * N_TILE)
 
         gain_bf = keep.tile([P, 1], BF16)
@@ -89,8 +110,6 @@ def tile_better_transformer_w_e_kernel(
         for v, vec in enumerate((bias, gamma, beta)):
             nc.scalar.dma_start(out=vec_rows[0:N_TILES, v, :], in_=vec.rearrange("(j p) -> j p", p=P))
 
-        ident_f32 = keep.tile([P, P], F32)
-        make_identity(nc, ident_f32[:])
         ident_bf = keep.tile([P, P], BF16)
         nc.vector.tensor_copy(out=ident_bf[:], in_=ident_f32[:])
         gain_f32 = keep.tile([P, 1], F32)
@@ -102,7 +121,7 @@ def tile_better_transformer_w_e_kernel(
         x_codes = keep.tile([P, GROUPS * P], U32, align_bytes=64)
         x_scales = keep.tile([P, GROUPS * P], U8, align_bytes=64)
         for pair in range(GROUPS // 2):
-            xt = psum_x.tile([P, 2, 2, P], F32, tag="xt")
+            xt = psum.tile([P, 2, 2, P], F32, tag="acc")
             for i in range(2):
                 g = 2 * pair + i
                 for u in range(2):
@@ -126,7 +145,7 @@ def tile_better_transformer_w_e_kernel(
                 in_=grouped[:].rearrange("p i c -> p (i c)"),
             )
 
-        vec_t = psum_x.tile([P, 3, P], BF16, tag="xt")
+        vec_t = psum_back.tile([P, 3, P], BF16, tag="back")
         for v in range(3):
             nc.tensor.transpose(vec_t[:, v, :], vec_rows[:, v, :], ident_bf[:])
         vec_cols = keep.tile([P, 3, N_TILES], F32)
@@ -146,25 +165,33 @@ def tile_better_transformer_w_e_kernel(
         mult_of = {}
         product_of = {}
 
+        def passes(t, i0, i1):
+            d0 = (t % TILES_PER_PART) * N_TILE
+            for i in range(i0, i1):
+                g = (t // TILES_PER_PART) * GROUPS_PER_PART + i
+                nc.tensor.matmul_mx(
+                    out=acc_of[t],
+                    lhsT=w_of[t, i].bitcast(FP8X4),
+                    lhsT_scale=planes[4 * (g % PLANES_PER_SET) : P, g // PLANES_PER_SET, d0 : d0 + N_TILE],
+                    rhs=x_codes[:, g * P : (g + 1) * P].bitcast(FP8X4),
+                    rhs_scale=x_scales[:, g * P : (g + 1) * P],
+                    start=(i == 0),
+                    stop=(i == GROUPS_PER_PART - 1),
+                )
+
         def multiply(k):
             first, count = units[k]
-            acc = psum_acc.tile([P, count, P], F32)
+            acc = psum.tile([P, UNIT_TILES, P], F32, tag="acc")
             for j in range(count):
-                t = first + j
-                w_sb, n0 = w_of[t]
-                d0 = (t % TILES_PER_PART) * N_TILE
-                for i in range(GROUPS_PER_PART):
-                    g = (t // TILES_PER_PART) * GROUPS_PER_PART + i
-                    nc.tensor.matmul_mx(
-                        out=acc[:, j, :],
-                        lhsT=w_sb[:, i, n0 : n0 + N_TILE].bitcast(FP8X4),
-                        lhsT_scale=planes[4 * (g % PLANES_PER_SET) : P, g // PLANES_PER_SET, d0 : d0 + N_TILE],
-                        rhs=x_codes[:, g * P : (g + 1) * P].bitcast(FP8X4),
-                        rhs_scale=x_scales[:, g * P : (g + 1) * P],
-                        start=(i == 0),
-                        stop=(i == GROUPS_PER_PART - 1),
-                    )
-            acc_of[k] = acc
+                acc_of[first + j] = acc[:, j, :]
+                passes(first + j, 0, GROUPS_PER_PART)
+
+        def multiply_last(half):
+            for t in range(FIRST_OF_LAST, N_TILES):
+                if half == 0:
+                    acc = psum.tile([P, UNIT_TILES, P], F32, tag="acc")
+                    acc_of[t] = acc[:, 0, :]
+                passes(t, half * HALF, (half + 1) * HALF)
 
         def squash(k):
             first, count = units[k]
@@ -173,7 +200,7 @@ def tile_better_transformer_w_e_kernel(
                 t = first + j
                 nc.scalar.activation(
                     out=mult[:, j, :],
-                    in_=acc_of[k][:, j, :],
+                    in_=acc_of[t],
                     func=ACT.Sigmoid,
                     scale=beta_col[:, t : t + 1],
                     bias=beta_bias_col[:, t : t + 1],
@@ -198,7 +225,7 @@ def tile_better_transformer_w_e_kernel(
                 t = first + j
                 nc.vector.scalar_tensor_tensor(
                     out=product[:, j, :],
-                    in0=acc_of[k][:, j, :],
+                    in0=acc_of[t],
                     scalar=bias_col[:, t : t + 1],
                     in1=mult[:, j, :],
                     op0=ALU.add,
@@ -208,24 +235,34 @@ def tile_better_transformer_w_e_kernel(
 
         def finish(k):
             first, count = units[k]
-            back = psum_back.tile([P, count * N_TILE], F32)
+            back = psum_back.tile([P, UNIT_TILES * N_TILE], F32, tag="back")
             for j in range(count):
                 nc.tensor.transpose(back[:, j * N_TILE : (j + 1) * N_TILE], product_of[k][:, j, :], ident_f32[:])
             out_sb, c0 = out_of[first]
             c1 = c0 + count * N_TILE
             f1 = (first + count) * N_TILE
             nc.vector.tensor_tensor(
-                out=out_sb[:, c0:c1], in0=back[:], in1=x_sb[:, first * N_TILE : f1], op=ALU.add
+                out=out_sb[:, c0:c1], in0=back[:, 0 : count * N_TILE], in1=x_sb[:, first * N_TILE : f1], op=ALU.add
             )
             if c1 == out_sb.shape[1]:
                 nc.sync.dma_start(out=out[:, f1 - c1 : f1], in_=out_sb[:])
 
-        for step in range(len(units) + 2):
-            if step < len(units):
-                multiply(step)
-            if 1 <= step <= len(units):
+        whole = len(units) - 2
+        for step in range(whole):
+            multiply(step)
+            if step >= 1:
                 gate(step - 1)
-            if step < len(units):
-                squash(step)
+            squash(step)
             if step >= 2:
                 finish(step - 2)
+        finish(whole - 2)
+        multiply_last(0)
+        gate(whole - 1)
+        finish(whole - 1)
+        multiply_last(1)
+        squash(whole)
+        squash(whole + 1)
+        gate(whole)
+        gate(whole + 1)
+        finish(whole)
+        finish(whole + 1)

@@ -63,18 +63,13 @@ def tile_better_transformer_w_e_kernel(
         x_sb = keep.tile([P, FEATURES], BF16)
         for e in range(PARTS):
             nc.sync.dma_start(out=x_sb[:, e * D : (e + 1) * D], in_=x[:, e * D : (e + 1) * D])
-        for s in range(PLANE_SETS - 1):
+        for s in range(PLANE_SETS):
+            queue, word = (nc.sync, I32) if s == 0 else (nc.gpsimd, F32)
             for q in range(4):
-                nc.sync.dma_start(
-                    out=planes[32 * q : 32 * q + 16, s, :].bitcast(I32),
-                    in_=w_scales[PLANES_PER_SET * s : PLANES_PER_SET * (s + 1), 4 * q : 4 * q + 4, :].bitcast(I32),
+                queue.dma_start(
+                    out=planes[32 * q : 32 * q + 16, s, :].bitcast(word),
+                    in_=w_scales[PLANES_PER_SET * s : PLANES_PER_SET * (s + 1), 4 * q : 4 * q + 4, :].bitcast(word),
                 )
-        s = PLANE_SETS - 1
-        for q in range(4):
-            nc.gpsimd.dma_start(
-                out=planes[32 * q : 32 * q + 16, s, :].bitcast(F32),
-                in_=w_scales[PLANES_PER_SET * s : PLANES_PER_SET * (s + 1), 4 * q : 4 * q + 4, :].bitcast(F32),
-            )
         w_of = {}
 
         def load_weights(first, count, i0, i1):

@@ -253,11 +253,11 @@ def tile_better_transformer_w_e_kernel(
         finish(whole - 2)
         multiply_last(0)
         gate(whole - 1)
-        finish(whole - 1)
         multiply_last(1)
         squash(whole)
         squash(whole + 1)
         gate(whole)
+        finish(whole - 1)
         gate(whole + 1)
         finish(whole)
         finish(whole + 1)

import concourse.mybir as mybir
from concourse.masks import make_identity

F32 = mybir.dt.float32
BF16 = mybir.dt.bfloat16
I32 = mybir.dt.int32
U32 = mybir.dt.uint32
U8 = mybir.dt.uint8
FP8X4 = mybir.dt.float8_e4m3fn_x4
ALU = mybir.AluOpType
ACT = mybir.ActivationFunctionType

P = 128
PARTS = 2
D = 3072
FEATURES = PARTS * D
K_PASS = 512
GROUPS_PER_PART = D // K_PASS
GROUPS = PARTS * GROUPS_PER_PART
WORDS_PER_GROUP = K_PASS // 2
N_TILE = 128
N_TILES = FEATURES // N_TILE
TILES_PER_PART = D // N_TILE
UNIT_TILES = 4
LOADS = (8, 8, 8, 8, 4, 4, 4)
LAST_TILES = 4
UNITS = (UNIT_TILES,) * 11 + (2, 2)
STORES = (32, 8, 4, 2, 2)
FIRST_OF_LAST = N_TILES - LAST_TILES
HALF = 3
PLANES_PER_SET = 4
PLANE_SETS = GROUPS // PLANES_PER_SET

FLOPS = 2 * P * D * D * PARTS


def starts_and_sizes(sizes):
    return [(sum(sizes[:i]), size) for i, size in enumerate(sizes)]


def tile_better_transformer_w_e_kernel(
    tc, x, weights_words, weights_scales, bias, gain, norm_bias, gamma, beta, out
):
    nc = tc.nc
    w_words = weights_words.rearrange("g p n t -> g p (n t)").bitcast(I32)
    w_scales = weights_scales

    loads = starts_and_sizes(LOADS)
    units = starts_and_sizes(UNITS)
    stores = starts_and_sizes(STORES)

    with tc.tile_pool(name="keep", bufs=1) as keep, tc.tile_pool(name="stage", bufs=2) as stage, tc.tile_pool(
        name="work", bufs=3
    ) as work, tc.psum_pool(name="psum", bufs=6) as psum, tc.psum_pool(
        name="psum_back", bufs=2
    ) as psum_back, tc.manual_schedule():
        ident_f32 = keep.tile([P, P], F32)
        make_identity(nc, ident_f32[:])

        planes = keep.tile([P, PLANE_SETS, D], U8, align_bytes=64)
        for s in range(PLANE_SETS):
            nc.vector.memset(planes[:, s, :].bitcast(I32), 0)
        x_sb = keep.tile([P, FEATURES], BF16)
        for e in range(PARTS):
            nc.sync.dma_start(out=x_sb[:, e * D : (e + 1) * D], in_=x[:, e * D : (e + 1) * D])
        for s in range(PLANE_SETS):
            queue, word = (nc.sync, I32) if s == 0 else (nc.gpsimd, F32)
            for q in range(4):
                queue.dma_start(
                    out=planes[32 * q : 32 * q + 16, s, :].bitcast(word),
                    in_=w_scales[PLANES_PER_SET * s : PLANES_PER_SET * (s + 1), 4 * q : 4 * q + 4, :].bitcast(word),
                )
        w_of = {}

        def load_weights(first, count, i0, i1):
            e = first // TILES_PER_PART
            d0 = (first % TILES_PER_PART) * N_TILE
            w_sb = keep.tile([P, i1 - i0, count * N_TILE], I32, name="w%d_%d" % (first, i0), align_bytes=64)
            nc.sync.dma_start(
                out=w_sb[:],
                in_=w_words[
                    e * GROUPS_PER_PART + i0 : e * GROUPS_PER_PART + i1, :, d0 : d0 + count * N_TILE
                ].rearrange("g p n -> p g n"),
            )
            for j in range(count):
                for i in range(i0, i1):
                    w_of[first + j, i] = w_sb[:, i - i0, j * N_TILE : (j + 1) * N_TILE]

        for first, count in loads:
            load_weights(first, count, 0, GROUPS_PER_PART)
        load_weights(FIRST_OF_LAST, LAST_TILES, 0, HALF)
        load_weights(FIRST_OF_LAST, LAST_TILES, HALF, GROUPS_PER_PART)
        out_of = {}
        for first, count in stores:
            out_sb = keep.tile([P, count * N_TILE], F32, name="out%d" % first)
            for t in range(first, first + count):
                out_of[t] = (out_sb, (t - first) * N_TILE)

        gain_bf = keep.tile([P, 1], BF16)
        nc.scalar.dma_start(out=gain_bf[:], in_=gain.partition_broadcast(P))
        shift_bf = keep.tile([P, 1], BF16)
        nc.scalar.dma_start(out=shift_bf[:], in_=norm_bias.partition_broadcast(P))
        vec_rows = keep.tile([P, 3, P], BF16)
        nc.vector.memset(vec_rows[:], 0.0)
        for v, vec in enumerate((bias, gamma, beta)):
            nc.scalar.dma_start(out=vec_rows[0:N_TILES, v, :], in_=vec.rearrange("(j p) -> j p", p=P))

        ident_bf = keep.tile([P, P], BF16)
        nc.vector.tensor_copy(out=ident_bf[:], in_=ident_f32[:])
        gain_f32 = keep.tile([P, 1], F32)
        nc.vector.tensor_copy(out=gain_f32[:], in_=gain_bf[:])
        shift_f32 = keep.tile([P, 1], F32)
        nc.vector.tensor_copy(out=shift_f32[:], in_=shift_bf[:])

        x_words = x_sb[:].bitcast(F32)
        x_codes = keep.tile([P, GROUPS * P], U32, align_bytes=64)
        x_scales = keep.tile([P, GROUPS * P], U8, align_bytes=64)
        for pair in range(GROUPS // 2):
            xt = psum.tile([P, 2, 2, P], F32, tag="acc")
            for i in range(2):
                g = 2 * pair + i
                for u in range(2):
                    nc.tensor.transpose(
                        xt[:, i, u, :],
                        x_words[:, WORDS_PER_GROUP * g + u : WORDS_PER_GROUP * (g + 1) : 2],
                        ident_f32[:],
                    )
            grouped = stage.tile([P, 2, K_PASS], BF16, align_bytes=64)
            for i in range(2):
                nc.scalar.activation(
                    out=grouped[:, i, :].rearrange("p (b u e) -> p b u e", u=2, e=2),
                    in_=xt[:, i, :, :].bitcast(BF16).rearrange("p u (b e) -> p b u e", e=2),
                    func=ACT.Identity,
                    scale=gain_f32[:, 0:1],
                    bias=shift_f32[:, 0:1],
                )
            nc.vector.quantize_mx(
                out=x_codes[:, 2 * P * pair : 2 * P * (pair + 1)].bitcast(FP8X4),
                scales=x_scales[:, 2 * P * pair : 2 * P * (pair + 1)],
                in_=grouped[:].rearrange("p i c -> p (i c)"),
            )

        vec_t = psum_back.tile([P, 3, P], BF16, tag="back")
        for v in range(3):
            nc.tensor.transpose(vec_t[:, v, :], vec_rows[:, v, :], ident_bf[:])
        vec_cols = keep.tile([P, 3, N_TILES], F32)
        nc.vector.tensor_copy(out=vec_cols[:], in_=vec_t[:, :, 0:N_TILES])
        bias_col = vec_cols[:, 0, :]
        gamma_col = vec_cols[:, 1, :]
        beta_col = vec_cols[:, 2, :]
        rest_col = keep.tile([P, N_TILES], F32)
        nc.vector.tensor_scalar(
            out=rest_col[:], in0=gamma_col, scalar1=-1.0, scalar2=1.0, op0=ALU.mult, op1=ALU.add
        )

        beta_bias_col = keep.tile([P, N_TILES], F32)
        nc.vector.tensor_tensor(out=beta_bias_col[:], in0=beta_col, in1=bias_col, op=ALU.mult)

        acc_of = {}
        mult_of = {}
        product_of = {}

        def passes(t, i0, i1):
            d0 = (t % TILES_PER_PART) * N_TILE
            for i in range(i0, i1):
                g = (t // TILES_PER_PART) * GROUPS_PER_PART + i
                nc.tensor.matmul_mx(
                    out=acc_of[t],
                    lhsT=w_of[t, i].bitcast(FP8X4),
                    lhsT_scale=planes[4 * (g % PLANES_PER_SET) : P, g // PLANES_PER_SET, d0 : d0 + N_TILE],
                    rhs=x_codes[:, g * P : (g + 1) * P].bitcast(FP8X4),
                    rhs_scale=x_scales[:, g * P : (g + 1) * P],
                    start=(i == 0),
                    stop=(i == GROUPS_PER_PART - 1),
                )

        def multiply(k):
            first, count = units[k]
            acc = psum.tile([P, UNIT_TILES, P], F32, tag="acc")
            for j in range(count):
                acc_of[first + j] = acc[:, j, :]
                passes(first + j, 0, GROUPS_PER_PART)

        def multiply_last(half):
            for t in range(FIRST_OF_LAST, N_TILES):
                if half == 0:
                    acc = psum.tile([P, UNIT_TILES, P], F32, tag="acc")
                    acc_of[t] = acc[:, 0, :]
                passes(t, half * HALF, (half + 1) * HALF)

        def squash(k):
            first, count = units[k]
            mult = work.tile([P, count, P], F32)
            for j in range(count):
                t = first + j
                nc.scalar.activation(
                    out=mult[:, j, :],
                    in_=acc_of[t],
                    func=ACT.Sigmoid,
                    scale=beta_col[:, t : t + 1],
                    bias=beta_bias_col[:, t : t + 1],
                )
            mult_of[k] = mult

        def gate(k):
            first, count = units[k]
            mult = mult_of[k]
            product = work.tile([P, count, P], F32)
            for j in range(count):
                t = first + j
                nc.vector.tensor_scalar(
                    out=mult[:, j, :],
                    in0=mult[:, j, :],
                    scalar1=rest_col[:, t : t + 1],
                    scalar2=gamma_col[:, t : t + 1],
                    op0=ALU.mult,
                    op1=ALU.add,
                )
            for j in range(count):
                t = first + j
                nc.vector.scalar_tensor_tensor(
                    out=product[:, j, :],
                    in0=acc_of[t],
                    scalar=bias_col[:, t : t + 1],
                    in1=mult[:, j, :],
                    op0=ALU.add,
                    op1=ALU.mult,
                )
            product_of[k] = product

        def finish(k):
            first, count = units[k]
            back = psum_back.tile([P, UNIT_TILES * N_TILE], F32, tag="back")
            for j in range(count):
                nc.tensor.transpose(back[:, j * N_TILE : (j + 1) * N_TILE], product_of[k][:, j, :], ident_f32[:])
            out_sb, c0 = out_of[first]
            c1 = c0 + count * N_TILE
            f1 = (first + count) * N_TILE
            nc.vector.tensor_tensor(
                out=out_sb[:, c0:c1], in0=back[:, 0 : count * N_TILE], in1=x_sb[:, first * N_TILE : f1], op=ALU.add
            )
            if c1 == out_sb.shape[1]:
                nc.sync.dma_start(out=out[:, f1 - c1 : f1], in_=out_sb[:])

        whole = len(units) - 2
        for step in range(whole):
            multiply(step)
            if step >= 1:
                gate(step - 1)
            squash(step)
            if step >= 2:
                finish(step - 2)
        finish(whole - 2)
        multiply_last(0)
        gate(whole - 1)
        multiply_last(1)
        squash(whole)
        squash(whole + 1)
        gate(whole)
        finish(whole - 1)
        gate(whole + 1)
        finish(whole)
        finish(whole + 1)
